import numpy as np
import ml_dtypes

BF16 = ml_dtypes.bfloat16


def bf(x):
    return np.asarray(x, np.float32).astype(BF16)


def f32(x):
    return np.asarray(x, np.float32)


def f64(x):
    return np.asarray(x).astype(np.float64)


def striped(idx):
    return np.tile(idx.reshape(-1, 16).T, (8, 1))


C, F, S, N, Q, BS, RK, NB, R, T = 1024, 1024, 4096, 2048, 256, 128, 128, 8, 2, 1024


def setup_inputs():
    return {
        "base": f32(np.random.standard_normal((C, S))),
        "x": bf(np.random.standard_normal((F, N))),
        "shared_in": bf(np.random.standard_normal((F, Q)) / np.sqrt(F)),
        "shared_out": bf(np.random.standard_normal((Q, C)) / np.sqrt(Q)),
        "rule_in": bf(np.random.standard_normal((R, BS, RK)) / np.sqrt(BS)),
        "rule_out": bf(np.random.standard_normal((R, RK, BS)) / np.sqrt(RK)),
        "logits": f32(np.random.standard_normal((R, NB)) / np.sqrt(NB)),
        "offs": striped(np.random.permutation(S)[:N]),
    }


def reference(base, x, shared_in, shared_out, rule_in, rule_out, logits, offs):
    idx = offs[:16].T.reshape(-1)
    xx = f64(x)
    low = f64(shared_in).T @ xx
    shared = f64(shared_out).T @ low
    e = np.exp(np.sqrt(NB) * f64(logits))
    sel = e / e.sum(axis=1, keepdims=True)
    weighted = np.empty((NB, BS, N))
    for r in range(R):
        xr = xx[:, r * T:(r + 1) * T].reshape(NB, BS, T)
        hid = f64(rule_in)[r].T @ xr
        ada = f64(rule_out)[r].T @ hid
        weighted[:, :, r * T:(r + 1) * T] = ada * sel[r][:, None, None]
    out = f64(base).copy()
    out[:, idx] = shared + weighted.reshape(C, N)
    return out

@@ -1,0 +1,124 @@
+import math
+
+import concourse.mybir as mybir
+
+BF16, F32, U16 = mybir.dt.bfloat16, mybir.dt.float32, mybir.dt.uint16
+ADD, SUBTRACT, MULT = mybir.AluOpType.add, mybir.AluOpType.subtract, mybir.AluOpType.mult
+COPY, EXP = mybir.ActivationFunctionType.Copy, mybir.ActivationFunctionType.Exp
+X_AXIS = mybir.AxisListType.X
+
+P = 128
+C, F, S, N, Q = 1024, 1024, 4096, 2048, 256
+R, NB = 2, 8
+QB = Q // P
+CHUNK = 512
+N_CHUNKS = N // CHUNK
+CHUNKS_PER_RULE = N_CHUNKS // R
+
+FLOPS = 2 * N * (F * Q + Q * C + 2 * NB * P * P)
+
+
+def tile_ruleawareprojection_b_kernel(
+    tc, base, x, shared_in, shared_out, rule_in, rule_out, logits, offs, out
+):
+    nc = tc.nc
+    x_blocks = x.rearrange("(k p) n -> k p n", p=P)
+    base_blocks = base.rearrange("(b p) s -> b p s", p=P)
+    out_blocks = out.rearrange("(b p) s -> b p s", p=P)
+
+    with (
+        tc.tile_pool(name="held", bufs=1) as held,
+        tc.tile_pool(name="terms", bufs=2) as terms,
+        tc.tile_pool(name="hidden", bufs=N_CHUNKS) as hidden,
+        tc.psum_pool(name="banks", bufs=8) as banks,
+    ):
+        offsets = held.tile([P, N // 16], U16, name="offsets")
+        nc.sync.dma_start(offsets[:], offs)
+
+        w_in = held.tile([P, NB, Q], BF16, name="w_in")
+        nc.scalar.dma_start(w_in[:], shared_in.rearrange("(k p) q -> p k q", p=P))
+        logit_rows = held.tile([P, R * NB], F32, name="logit_rows")
+        nc.scalar.dma_start(logit_rows[:], logits.rearrange("r b -> (r b)").partition_broadcast(P))
+        a_in = held.tile([P, R, P], BF16, name="a_in")
+        nc.scalar.dma_start(a_in[:], rule_in.rearrange("r v k -> v r k"))
+        a_out = held.tile([P, R, P], BF16, name="a_out")
+        nc.scalar.dma_start(a_out[:], rule_out.rearrange("r k u -> k r u"))
+        w_out = held.tile([P, QB, C], BF16, name="w_out")
+        nc.scalar.dma_start(w_out[:], shared_out.rearrange("(q p) c -> p q c", p=P))
+
+        x_sb = []
+        for t in range(N_CHUNKS):
+            x_sb.append([])
+            for k in range(NB):
+                x_tk = held.tile([P, CHUNK], BF16, name=f"x_{t}_{k}")
+                nc.sync.dma_start(x_tk[:], x_blocks[k][:, t * CHUNK : (t + 1) * CHUNK])
+                x_sb[t].append(x_tk)
+
+        window = []
+        for b in range(NB):
+            window_b = held.tile([P, S], F32, name=f"window_{b}")
+            nc.sync.dma_start(window_b[:], base_blocks[b])
+            window.append(window_b)
+
+        logit_rb = logit_rows[:].rearrange("p (r b) -> p r b", r=R)
+        top = held.tile([P, R], F32, name="top")
+        nc.vector.reduce_max(top[:], logit_rb, axis=X_AXIS)
+        shifted = held.tile([P, R, NB], F32, name="shifted")
+        nc.vector.tensor_tensor(shifted[:], logit_rb, top[:].unsqueeze(2).to_broadcast([P, R, NB]), SUBTRACT)
+        grown = held.tile([P, R, NB], F32, name="grown")
+        nc.scalar.activation(grown[:], shifted[:], EXP, scale=math.sqrt(NB))
+        total = held.tile([P, R], F32, name="total")
+        nc.vector.reduce_sum(total[:], grown[:], axis=X_AXIS)
+        inverse = held.tile([P, R], F32, name="inverse")
+        nc.vector.reciprocal(inverse[:], total[:])
+        sel = held.tile([P, R, NB], F32, name="sel")
+        nc.vector.tensor_tensor(sel[:], grown[:], inverse[:].unsqueeze(2).to_broadcast([P, R, NB]), MULT)
+
+        low_sb = []
+        for t in range(N_CHUNKS):
+            low_sb.append([])
+            for q in range(QB):
+                low_ps = banks.tile([P, CHUNK], F32, name="low_ps", tag="bank")
+                for k in range(NB):
+                    nc.tensor.matmul(
+                        low_ps[:],
+                        w_in[:, k, q * P : (q + 1) * P],
+                        x_sb[t][k][:],
+                        start=(k == 0),
+                        stop=(k == NB - 1),
+                    )
+                low_tq = held.tile([P, CHUNK], BF16, name=f"low_{t}_{q}")
+                nc.vector.tensor_copy(low_tq[:], low_ps[:])
+                low_sb[t].append(low_tq)
+
+        for b in range(NB):
+            channels = slice(b * P, (b + 1) * P)
+            shared_sb = terms.tile([P, N], F32, name="shared_sb")
+            weighted_sb = terms.tile([P, N], F32, name="weighted_sb")
+
+            hid_sb = []
+            for t in range(N_CHUNKS):
+                hid_ps = banks.tile([P, CHUNK], F32, name="hid_ps", tag="bank")
+                nc.tensor.matmul(hid_ps[:], a_in[:, t // CHUNKS_PER_RULE, :], x_sb[t][b][:], start=True, stop=True)
+                hid_t = hidden.tile([P, CHUNK], BF16, name="hid_t")
+                nc.scalar.copy(hid_t[:], hid_ps[:])
+                hid_sb.append(hid_t)
+
+            for t in range(N_CHUNKS):
+                shared_ps = banks.tile([P, CHUNK], F32, name="shared_ps", tag="bank")
+                for q in range(QB):
+                    nc.tensor.matmul(
+                        shared_ps[:], w_out[:, q, channels], low_sb[t][q][:], start=(q == 0), stop=(q == QB - 1)
+                    )
+                nc.scalar.copy(shared_sb[:, t * CHUNK : (t + 1) * CHUNK], shared_ps[:])
+
+            for t in range(N_CHUNKS):
+                r = t // CHUNKS_PER_RULE
+                ada_ps = banks.tile([P, CHUNK], F32, name="ada_ps", tag="bank")
+                nc.tensor.matmul(ada_ps[:], a_out[:, r, :], hid_sb[t][:], start=True, stop=True)
+                nc.scalar.activation(
+                    weighted_sb[:, t * CHUNK : (t + 1) * CHUNK], ada_ps[:], COPY, scale=sel[:, r, b : b + 1]
+                )
+
+            nc.vector.tensor_tensor(window[b][:].indirect(offsets[:]), shared_sb[:], weighted_sb[:], ADD)
+            nc.sync.dma_start(out_blocks[b], window[b][:])

@@ -74,9 +74,12 @@ def tile_ruleawareprojection_b_kernel(
         sel = held.tile([P, R, NB], F32, name="sel")
         nc.vector.tensor_tensor(sel[:], grown[:], inverse[:].unsqueeze(2).to_broadcast([P, R, NB]), MULT)
 
-        low_sb = []
-        for t in range(N_CHUNKS):
-            low_sb.append([])
+        low_sb = {}
+        hid_sb = {}
+        shared_sb = {}
+        weighted_sb = {}
+
+        def make_low(t):
             for q in range(QB):
                 low_ps = banks.tile([P, CHUNK], F32, name="low_ps", tag="bank")
                 for k in range(NB):
@@ -87,38 +90,51 @@ def tile_ruleawareprojection_b_kernel(
                         start=(k == 0),
                         stop=(k == NB - 1),
                     )
-                low_tq = held.tile([P, CHUNK], BF16, name=f"low_{t}_{q}")
-                nc.vector.tensor_copy(low_tq[:], low_ps[:])
-                low_sb[t].append(low_tq)
+                low_sb[t, q] = held.tile([P, CHUNK], BF16, name=f"low_{t}_{q}")
+                nc.vector.tensor_copy(low_sb[t, q][:], low_ps[:])
+
+        def make_hid(b, t):
+            hid_ps = banks.tile([P, CHUNK], F32, name="hid_ps", tag="bank")
+            nc.tensor.matmul(hid_ps[:], a_in[:, t // CHUNKS_PER_RULE, :], x_sb[t][b][:], start=True, stop=True)
+            hid_sb[b, t] = hidden.tile([P, CHUNK], BF16, name="hid_t")
+            nc.scalar.copy(hid_sb[b, t][:], hid_ps[:])
+
+        def make_weighted(b, t):
+            r = t // CHUNKS_PER_RULE
+            ada_ps = banks.tile([P, CHUNK], F32, name="ada_ps", tag="bank")
+            nc.tensor.matmul(ada_ps[:], a_out[:, r, :], hid_sb[b, t][:], start=True, stop=True)
+            nc.scalar.activation(
+                weighted_sb[b][:, t * CHUNK : (t + 1) * CHUNK], ada_ps[:], COPY, scale=sel[:, r, b : b + 1]
+            )
+
+        def make_shared(b, t):
+            shared_ps = banks.tile([P, CHUNK], F32, name="shared_ps", tag="bank")
+            for q in range(QB):
+                nc.tensor.matmul(
+                    shared_ps[:],
+                    w_out[:, q, b * P : (b + 1) * P],
+                    low_sb[t, q][:],
+                    start=(q == 0),
+                    stop=(q == QB - 1),
+                )
+            nc.scalar.copy(shared_sb[b][:, t * CHUNK : (t + 1) * CHUNK], shared_ps[:])
 
         for b in range(NB):
-            channels = slice(b * P, (b + 1) * P)
-            shared_sb = terms.tile([P, N], F32, name="shared_sb")
-            weighted_sb = terms.tile([P, N], F32, name="weighted_sb")
+            shared_sb[b] = terms.tile([P, N], F32, name="shared_sb")
+            weighted_sb[b] = terms.tile([P, N], F32, name="weighted_sb")
+            if b == 0:
+                for t in range(N_CHUNKS):
+                    make_hid(b, t)
+                    make_low(t)
+                    make_weighted(b, t)
+                    make_shared(b, t)
+            else:
+                for t in range(N_CHUNKS):
+                    make_hid(b, t)
+                for t in range(N_CHUNKS):
+                    make_shared(b, t)
+                for t in range(N_CHUNKS):
+                    make_weighted(b, t)
 
-            hid_sb = []
-            for t in range(N_CHUNKS):
-                hid_ps = banks.tile([P, CHUNK], F32, name="hid_ps", tag="bank")
-                nc.tensor.matmul(hid_ps[:], a_in[:, t // CHUNKS_PER_RULE, :], x_sb[t][b][:], start=True, stop=True)
-                hid_t = hidden.tile([P, CHUNK], BF16, name="hid_t")
-                nc.scalar.copy(hid_t[:], hid_ps[:])
-                hid_sb.append(hid_t)
-
-            for t in range(N_CHUNKS):
-                shared_ps = banks.tile([P, CHUNK], F32, name="shared_ps", tag="bank")
-                for q in range(QB):
-                    nc.tensor.matmul(
-                        shared_ps[:], w_out[:, q, channels], low_sb[t][q][:], start=(q == 0), stop=(q == QB - 1)
-                    )
-                nc.scalar.copy(shared_sb[:, t * CHUNK : (t + 1) * CHUNK], shared_ps[:])
-
-            for t in range(N_CHUNKS):
-                r = t // CHUNKS_PER_RULE
-                ada_ps = banks.tile([P, CHUNK], F32, name="ada_ps", tag="bank")
-                nc.tensor.matmul(ada_ps[:], a_out[:, r, :], hid_sb[t][:], start=True, stop=True)
-                nc.scalar.activation(
-                    weighted_sb[:, t * CHUNK : (t + 1) * CHUNK], ada_ps[:], COPY, scale=sel[:, r, b : b + 1]
-                )
-
-            nc.vector.tensor_tensor(window[b][:].indirect(offsets[:]), shared_sb[:], weighted_sb[:], ADD)
+            nc.vector.tensor_tensor(window[b][:].indirect(offsets[:]), shared_sb[b][:], weighted_sb[b][:], ADD)
             nc.sync.dma_start(out_blocks[b], window[b][:])

@@ -35,12 +35,12 @@ def tile_ruleawareprojection_b_kernel(
         offsets = held.tile([P, N // 16], U16, name="offsets")
         nc.sync.dma_start(offsets[:], offs)
 
+        a_in = held.tile([P, R, P], BF16, name="a_in")
+        nc.scalar.dma_start(a_in[:], rule_in.rearrange("r v k -> v r k"))
         w_in = held.tile([P, NB, Q], BF16, name="w_in")
         nc.scalar.dma_start(w_in[:], shared_in.rearrange("(k p) q -> p k q", p=P))
         logit_rows = held.tile([P, R * NB], F32, name="logit_rows")
         nc.scalar.dma_start(logit_rows[:], logits.rearrange("r b -> (r b)").partition_broadcast(P))
-        a_in = held.tile([P, R, P], BF16, name="a_in")
-        nc.scalar.dma_start(a_in[:], rule_in.rearrange("r v k -> v r k"))
         a_out = held.tile([P, R, P], BF16, name="a_out")
         nc.scalar.dma_start(a_out[:], rule_out.rearrange("r k u -> k r u"))
         w_out = held.tile([P, QB, C], BF16, name="w_out")
@@ -117,17 +117,20 @@ def tile_ruleawareprojection_b_kernel(
                     start=(q == 0),
                     stop=(q == QB - 1),
                 )
-            nc.scalar.copy(shared_sb[b][:, t * CHUNK : (t + 1) * CHUNK], shared_ps[:])
+            copy_out = nc.vector.tensor_copy if b == 0 else nc.scalar.copy
+            copy_out(shared_sb[b][:, t * CHUNK : (t + 1) * CHUNK], shared_ps[:])
 
         for b in range(NB):
             shared_sb[b] = terms.tile([P, N], F32, name="shared_sb")
             weighted_sb[b] = terms.tile([P, N], F32, name="weighted_sb")
             if b == 0:
-                for t in range(N_CHUNKS):
-                    make_hid(b, t)
-                    make_low(t)
-                    make_weighted(b, t)
-                    make_shared(b, t)
+                for t in range(N_CHUNKS + 1):
+                    if t < N_CHUNKS:
+                        make_hid(b, t)
+                        make_low(t)
+                    if t > 0:
+                        make_weighted(b, t - 1)
+                        make_shared(b, t - 1)
             else:
                 for t in range(N_CHUNKS):
                     make_hid(b, t)

@@ -37,8 +37,11 @@ def tile_ruleawareprojection_b_kernel(
 
         a_in = held.tile([P, R, P], BF16, name="a_in")
         nc.scalar.dma_start(a_in[:], rule_in.rearrange("r v k -> v r k"))
-        w_in = held.tile([P, NB, Q], BF16, name="w_in")
-        nc.scalar.dma_start(w_in[:], shared_in.rearrange("(k p) q -> p k q", p=P))
+        w_in = []
+        for k in range(NB):
+            w_in_k = held.tile([P, Q], BF16, name=f"w_in_{k}")
+            nc.scalar.dma_start(w_in_k[:], shared_in[k * P : (k + 1) * P, :])
+            w_in.append(w_in_k)
         logit_rows = held.tile([P, R * NB], F32, name="logit_rows")
         nc.scalar.dma_start(logit_rows[:], logits.rearrange("r b -> (r b)").partition_broadcast(P))
         a_out = held.tile([P, R, P], BF16, name="a_out")
@@ -80,18 +83,19 @@ def tile_ruleawareprojection_b_kernel(
         weighted_sb = {}
 
         def make_low(t):
-            for q in range(QB):
-                low_ps = banks.tile([P, CHUNK], F32, name="low_ps", tag="bank")
-                for k in range(NB):
+            low_ps = [banks.tile([P, CHUNK], F32, name=f"low_ps_{q}", tag="bank") for q in range(QB)]
+            for k in range(NB):
+                for q in range(QB):
                     nc.tensor.matmul(
-                        low_ps[:],
-                        w_in[:, k, q * P : (q + 1) * P],
+                        low_ps[q][:],
+                        w_in[k][:, q * P : (q + 1) * P],
                         x_sb[t][k][:],
                         start=(k == 0),
                         stop=(k == NB - 1),
                     )
+            for q, copy_out in enumerate((nc.vector.tensor_copy, nc.scalar.copy)):
                 low_sb[t, q] = held.tile([P, CHUNK], BF16, name=f"low_{t}_{q}")
-                nc.vector.tensor_copy(low_sb[t, q][:], low_ps[:])
+                copy_out(low_sb[t, q][:], low_ps[q][:])
 
         def make_hid(b, t):
             hid_ps = banks.tile([P, CHUNK], F32, name="hid_ps", tag="bank")

@@ -14,6 +14,7 @@ QB = Q // P
 CHUNK = 512
 N_CHUNKS = N // CHUNK
 CHUNKS_PER_RULE = N_CHUNKS // R
+HALF = CHUNK // 2
 
 FLOPS = 2 * N * (F * Q + Q * C + 2 * NB * P * P)
 
@@ -121,8 +122,21 @@ def tile_ruleawareprojection_b_kernel(
                     start=(q == 0),
                     stop=(q == QB - 1),
                 )
-            copy_out = nc.vector.tensor_copy if b == 0 else nc.scalar.copy
-            copy_out(shared_sb[b][:, t * CHUNK : (t + 1) * CHUNK], shared_ps[:])
+            nc.scalar.copy(shared_sb[b][:, t * CHUNK : (t + 1) * CHUNK], shared_ps[:])
+
+        def make_shared_in_halves(b, t):
+            for h, copy_out in enumerate((nc.scalar.copy, nc.vector.tensor_copy)):
+                half_ps = banks.tile([P, HALF], F32, name="half_ps", tag="bank")
+                for q in range(QB):
+                    nc.tensor.matmul(
+                        half_ps[:],
+                        w_out[:, q, b * P : (b + 1) * P],
+                        low_sb[t, q][:, h * HALF : (h + 1) * HALF],
+                        start=(q == 0),
+                        stop=(q == QB - 1),
+                    )
+                first = t * CHUNK + h * HALF
+                copy_out(shared_sb[b][:, first : first + HALF], half_ps[:])
 
         for b in range(NB):
             shared_sb[b] = terms.tile([P, N], F32, name="shared_sb")
@@ -134,7 +148,7 @@ def tile_ruleawareprojection_b_kernel(
                         make_low(t)
                     if t > 0:
                         make_weighted(b, t - 1)
-                        make_shared(b, t - 1)
+                        make_shared_in_halves(b, t - 1)
             else:
                 for t in range(N_CHUNKS):
                     make_hid(b, t)

@@ -15,6 +15,8 @@ CHUNK = 512
 N_CHUNKS = N // CHUNK
 CHUNKS_PER_RULE = N_CHUNKS // R
 HALF = CHUNK // 2
+WHOLE = [slice(0, CHUNK)]
+HALVES = [slice(0, HALF), slice(HALF, CHUNK)]
 
 FLOPS = 2 * N * (F * Q + Q * C + 2 * NB * P * P)
 
@@ -33,11 +35,11 @@ def tile_ruleawareprojection_b_kernel(
         tc.tile_pool(name="hidden", bufs=N_CHUNKS) as hidden,
         tc.psum_pool(name="banks", bufs=8) as banks,
     ):
-        offsets = held.tile([P, N // 16], U16, name="offsets")
-        nc.sync.dma_start(offsets[:], offs)
-
-        a_in = held.tile([P, R, P], BF16, name="a_in")
-        nc.scalar.dma_start(a_in[:], rule_in.rearrange("r v k -> v r k"))
+        a_in = []
+        for r in range(R):
+            a_in_r = held.tile([P, P], BF16, name=f"a_in_{r}")
+            a_in.append(a_in_r)
+        nc.scalar.dma_start(a_in[0][:], rule_in[0])
         w_in = []
         for k in range(NB):
             w_in_k = held.tile([P, Q], BF16, name=f"w_in_{k}")
@@ -49,14 +51,19 @@ def tile_ruleawareprojection_b_kernel(
         nc.scalar.dma_start(a_out[:], rule_out.rearrange("r k u -> k r u"))
         w_out = held.tile([P, QB, C], BF16, name="w_out")
         nc.scalar.dma_start(w_out[:], shared_out.rearrange("(q p) c -> p q c", p=P))
+        nc.scalar.dma_start(a_in[1][:], rule_in[1])
 
         x_sb = []
         for t in range(N_CHUNKS):
             x_sb.append([])
             for k in range(NB):
                 x_tk = held.tile([P, CHUNK], BF16, name=f"x_{t}_{k}")
-                nc.sync.dma_start(x_tk[:], x_blocks[k][:, t * CHUNK : (t + 1) * CHUNK])
+                x_dram = x_blocks[k][:, t * CHUNK : (t + 1) * CHUNK]
+                for cols in HALVES if (t, k) == (0, 0) else WHOLE:
+                    nc.sync.dma_start(x_tk[:, cols], x_dram[:, cols])
                 x_sb[t].append(x_tk)
+        offsets = held.tile([P, N // 16], U16, name="offsets")
+        nc.sync.dma_start(offsets[:], offs)
 
         window = []
         for b in range(NB):
@@ -100,7 +107,10 @@ def tile_ruleawareprojection_b_kernel(
 
         def make_hid(b, t):
             hid_ps = banks.tile([P, CHUNK], F32, name="hid_ps", tag="bank")
-            nc.tensor.matmul(hid_ps[:], a_in[:, t // CHUNKS_PER_RULE, :], x_sb[t][b][:], start=True, stop=True)
+            for cols in HALVES if (b, t) == (0, 0) else WHOLE:
+                nc.tensor.matmul(
+                    hid_ps[:, cols], a_in[t // CHUNKS_PER_RULE][:], x_sb[t][b][:, cols], start=True, stop=True
+                )
             hid_sb[b, t] = hidden.tile([P, CHUNK], BF16, name="hid_t")
             nc.scalar.copy(hid_sb[b, t][:], hid_ps[:])
 
@@ -112,7 +122,7 @@ def tile_ruleawareprojection_b_kernel(
                 weighted_sb[b][:, t * CHUNK : (t + 1) * CHUNK], ada_ps[:], COPY, scale=sel[:, r, b : b + 1]
             )
 
-        def make_shared(b, t):
+        def make_shared(b, t, copy_out):
             shared_ps = banks.tile([P, CHUNK], F32, name="shared_ps", tag="bank")
             for q in range(QB):
                 nc.tensor.matmul(
@@ -122,7 +132,7 @@ def tile_ruleawareprojection_b_kernel(
                     start=(q == 0),
                     stop=(q == QB - 1),
                 )
-            nc.scalar.copy(shared_sb[b][:, t * CHUNK : (t + 1) * CHUNK], shared_ps[:])
+            copy_out(shared_sb[b][:, t * CHUNK : (t + 1) * CHUNK], shared_ps[:])
 
         def make_shared_in_halves(b, t):
             for h, copy_out in enumerate((nc.scalar.copy, nc.vector.tensor_copy)):
@@ -148,12 +158,15 @@ def tile_ruleawareprojection_b_kernel(
                         make_low(t)
                     if t > 0:
                         make_weighted(b, t - 1)
-                        make_shared_in_halves(b, t - 1)
+                        if t < N_CHUNKS:
+                            make_shared(b, t - 1, nc.vector.tensor_copy)
+                        else:
+                            make_shared_in_halves(b, t - 1)
             else:
                 for t in range(N_CHUNKS):
                     make_hid(b, t)
                 for t in range(N_CHUNKS):
-                    make_shared(b, t)
+                    make_shared(b, t, nc.scalar.copy)
                 for t in range(N_CHUNKS):
                     make_weighted(b, t)
 

@@ -17,6 +17,7 @@ CHUNKS_PER_RULE = N_CHUNKS // R
 HALF = CHUNK // 2
 WHOLE = [slice(0, CHUNK)]
 HALVES = [slice(0, HALF), slice(HALF, CHUNK)]
+LAST_PIECES = [(0, HALF), (HALF, HALF + HALF // 2), (HALF + HALF // 2, CHUNK)]
 
 FLOPS = 2 * N * (F * Q + Q * C + 2 * NB * P * P)
 
@@ -30,8 +31,9 @@ def tile_ruleawareprojection_b_kernel(
     out_blocks = out.rearrange("(b p) s -> b p s", p=P)
 
     with (
-        tc.tile_pool(name="held", bufs=1) as held,
+        tc.tile_pool(name="windows", bufs=1) as windows,
         tc.tile_pool(name="terms", bufs=2) as terms,
+        tc.tile_pool(name="held", bufs=1) as held,
         tc.tile_pool(name="hidden", bufs=N_CHUNKS) as hidden,
         tc.psum_pool(name="banks", bufs=8) as banks,
     ):
@@ -67,7 +69,7 @@ def tile_ruleawareprojection_b_kernel(
 
         window = []
         for b in range(NB):
-            window_b = held.tile([P, S], F32, name=f"window_{b}")
+            window_b = windows.tile([P, S], F32, name=f"window_{b}")
             nc.sync.dma_start(window_b[:], base_blocks[b])
             window.append(window_b)
 
@@ -134,19 +136,19 @@ def tile_ruleawareprojection_b_kernel(
                 )
             copy_out(shared_sb[b][:, t * CHUNK : (t + 1) * CHUNK], shared_ps[:])
 
-        def make_shared_in_halves(b, t):
-            for h, copy_out in enumerate((nc.scalar.copy, nc.vector.tensor_copy)):
-                half_ps = banks.tile([P, HALF], F32, name="half_ps", tag="bank")
+        def make_shared_in_pieces(b, t):
+            copies = (nc.scalar.copy, nc.vector.tensor_copy, nc.vector.tensor_copy)
+            for (first, last), copy_out in zip(LAST_PIECES, copies):
+                piece_ps = banks.tile([P, last - first], F32, name="piece_ps", tag="bank")
                 for q in range(QB):
                     nc.tensor.matmul(
-                        half_ps[:],
+                        piece_ps[:],
                         w_out[:, q, b * P : (b + 1) * P],
-                        low_sb[t, q][:, h * HALF : (h + 1) * HALF],
+                        low_sb[t, q][:, first:last],
                         start=(q == 0),
                         stop=(q == QB - 1),
                     )
-                first = t * CHUNK + h * HALF
-                copy_out(shared_sb[b][:, first : first + HALF], half_ps[:])
+                copy_out(shared_sb[b][:, t * CHUNK + first : t * CHUNK + last], piece_ps[:])
 
         for b in range(NB):
             shared_sb[b] = terms.tile([P, N], F32, name="shared_sb")
@@ -161,7 +163,7 @@ def tile_ruleawareprojection_b_kernel(
                         if t < N_CHUNKS:
                             make_shared(b, t - 1, nc.vector.tensor_copy)
                         else:
-                            make_shared_in_halves(b, t - 1)
+                            make_shared_in_pieces(b, t - 1)
             else:
                 for t in range(N_CHUNKS):
                     make_hid(b, t)

import math

import concourse.mybir as mybir

BF16, F32, U16 = mybir.dt.bfloat16, mybir.dt.float32, mybir.dt.uint16
ADD, SUBTRACT, MULT = mybir.AluOpType.add, mybir.AluOpType.subtract, mybir.AluOpType.mult
COPY, EXP = mybir.ActivationFunctionType.Copy, mybir.ActivationFunctionType.Exp
X_AXIS = mybir.AxisListType.X

P = 128
C, F, S, N, Q = 1024, 1024, 4096, 2048, 256
R, NB = 2, 8
QB = Q // P
CHUNK = 512
N_CHUNKS = N // CHUNK
CHUNKS_PER_RULE = N_CHUNKS // R
HALF = CHUNK // 2
WHOLE = [slice(0, CHUNK)]
HALVES = [slice(0, HALF), slice(HALF, CHUNK)]
LAST_PIECES = [(0, HALF), (HALF, HALF + HALF // 2), (HALF + HALF // 2, CHUNK)]

FLOPS = 2 * N * (F * Q + Q * C + 2 * NB * P * P)


def tile_ruleawareprojection_b_kernel(
    tc, base, x, shared_in, shared_out, rule_in, rule_out, logits, offs, out
):
    nc = tc.nc
    x_blocks = x.rearrange("(k p) n -> k p n", p=P)
    base_blocks = base.rearrange("(b p) s -> b p s", p=P)
    out_blocks = out.rearrange("(b p) s -> b p s", p=P)

    with (
        tc.tile_pool(name="windows", bufs=1) as windows,
        tc.tile_pool(name="terms", bufs=2) as terms,
        tc.tile_pool(name="held", bufs=1) as held,
        tc.tile_pool(name="hidden", bufs=N_CHUNKS) as hidden,
        tc.psum_pool(name="banks", bufs=8) as banks,
    ):
        a_in = []
        for r in range(R):
            a_in_r = held.tile([P, P], BF16, name=f"a_in_{r}")
            a_in.append(a_in_r)
        nc.scalar.dma_start(a_in[0][:], rule_in[0])
        w_in = []
        for k in range(NB):
            w_in_k = held.tile([P, Q], BF16, name=f"w_in_{k}")
            nc.scalar.dma_start(w_in_k[:], shared_in[k * P : (k + 1) * P, :])
            w_in.append(w_in_k)
        logit_rows = held.tile([P, R * NB], F32, name="logit_rows")
        nc.scalar.dma_start(logit_rows[:], logits.rearrange("r b -> (r b)").partition_broadcast(P))
        a_out = held.tile([P, R, P], BF16, name="a_out")
        nc.scalar.dma_start(a_out[:], rule_out.rearrange("r k u -> k r u"))
        w_out = held.tile([P, QB, C], BF16, name="w_out")
        nc.scalar.dma_start(w_out[:], shared_out.rearrange("(q p) c -> p q c", p=P))
        nc.scalar.dma_start(a_in[1][:], rule_in[1])

        x_sb = []
        for t in range(N_CHUNKS):
            x_sb.append([])
            for k in range(NB):
                x_tk = held.tile([P, CHUNK], BF16, name=f"x_{t}_{k}")
                x_dram = x_blocks[k][:, t * CHUNK : (t + 1) * CHUNK]
                for cols in HALVES if (t, k) == (0, 0) else WHOLE:
                    nc.sync.dma_start(x_tk[:, cols], x_dram[:, cols])
                x_sb[t].append(x_tk)
        offsets = held.tile([P, N // 16], U16, name="offsets")
        nc.sync.dma_start(offsets[:], offs)

        window = []
        for b in range(NB):
            window_b = windows.tile([P, S], F32, name=f"window_{b}")
            nc.sync.dma_start(window_b[:], base_blocks[b])
            window.append(window_b)

        logit_rb = logit_rows[:].rearrange("p (r b) -> p r b", r=R)
        top = held.tile([P, R], F32, name="top")
        nc.vector.reduce_max(top[:], logit_rb, axis=X_AXIS)
        shifted = held.tile([P, R, NB], F32, name="shifted")
        nc.vector.tensor_tensor(shifted[:], logit_rb, top[:].unsqueeze(2).to_broadcast([P, R, NB]), SUBTRACT)
        grown = held.tile([P, R, NB], F32, name="grown")
        nc.scalar.activation(grown[:], shifted[:], EXP, scale=math.sqrt(NB))
        total = held.tile([P, R], F32, name="total")
        nc.vector.reduce_sum(total[:], grown[:], axis=X_AXIS)
        inverse = held.tile([P, R], F32, name="inverse")
        nc.vector.reciprocal(inverse[:], total[:])
        sel = held.tile([P, R, NB], F32, name="sel")
        nc.vector.tensor_tensor(sel[:], grown[:], inverse[:].unsqueeze(2).to_broadcast([P, R, NB]), MULT)

        low_sb = {}
        hid_sb = {}
        shared_sb = {}
        weighted_sb = {}

        def make_low(t):
            low_ps = [banks.tile([P, CHUNK], F32, name=f"low_ps_{q}", tag="bank") for q in range(QB)]
            for k in range(NB):
                for q in range(QB):
                    nc.tensor.matmul(
                        low_ps[q][:],
                        w_in[k][:, q * P : (q + 1) * P],
                        x_sb[t][k][:],
                        start=(k == 0),
                        stop=(k == NB - 1),
                    )
            for q, copy_out in enumerate((nc.vector.tensor_copy, nc.scalar.copy)):
                low_sb[t, q] = held.tile([P, CHUNK], BF16, name=f"low_{t}_{q}")
                copy_out(low_sb[t, q][:], low_ps[q][:])

        def make_hid(b, t):
            hid_ps = banks.tile([P, CHUNK], F32, name="hid_ps", tag="bank")
            for cols in HALVES if (b, t) == (0, 0) else WHOLE:
                nc.tensor.matmul(
                    hid_ps[:, cols], a_in[t // CHUNKS_PER_RULE][:], x_sb[t][b][:, cols], start=True, stop=True
                )
            hid_sb[b, t] = hidden.tile([P, CHUNK], BF16, name="hid_t")
            nc.scalar.copy(hid_sb[b, t][:], hid_ps[:])

        def make_weighted(b, t):
            r = t // CHUNKS_PER_RULE
            ada_ps = banks.tile([P, CHUNK], F32, name="ada_ps", tag="bank")
            nc.tensor.matmul(ada_ps[:], a_out[:, r, :], hid_sb[b, t][:], start=True, stop=True)
            nc.scalar.activation(
                weighted_sb[b][:, t * CHUNK : (t + 1) * CHUNK], ada_ps[:], COPY, scale=sel[:, r, b : b + 1]
            )

        def make_shared(b, t, copy_out):
            shared_ps = banks.tile([P, CHUNK], F32, name="shared_ps", tag="bank")
            for q in range(QB):
                nc.tensor.matmul(
                    shared_ps[:],
                    w_out[:, q, b * P : (b + 1) * P],
                    low_sb[t, q][:],
                    start=(q == 0),
                    stop=(q == QB - 1),
                )
            copy_out(shared_sb[b][:, t * CHUNK : (t + 1) * CHUNK], shared_ps[:])

        def make_shared_in_pieces(b, t):
            copies = (nc.scalar.copy, nc.vector.tensor_copy, nc.vector.tensor_copy)
            for (first, last), copy_out in zip(LAST_PIECES, copies):
                piece_ps = banks.tile([P, last - first], F32, name="piece_ps", tag="bank")
                for q in range(QB):
                    nc.tensor.matmul(
                        piece_ps[:],
                        w_out[:, q, b * P : (b + 1) * P],
                        low_sb[t, q][:, first:last],
                        start=(q == 0),
                        stop=(q == QB - 1),
                    )
                copy_out(shared_sb[b][:, t * CHUNK + first : t * CHUNK + last], piece_ps[:])

        for b in range(NB):
            shared_sb[b] = terms.tile([P, N], F32, name="shared_sb")
            weighted_sb[b] = terms.tile([P, N], F32, name="weighted_sb")
            if b == 0:
                for t in range(N_CHUNKS + 1):
                    if t < N_CHUNKS:
                        make_hid(b, t)
                        make_low(t)
                    if t > 0:
                        make_weighted(b, t - 1)
                        if t < N_CHUNKS:
                            make_shared(b, t - 1, nc.vector.tensor_copy)
                        else:
                            make_shared_in_pieces(b, t - 1)
            else:
                for t in range(N_CHUNKS):
                    make_hid(b, t)
                for t in range(N_CHUNKS):
                    make_shared(b, t, nc.scalar.copy)
                for t in range(N_CHUNKS):
                    make_weighted(b, t)

            nc.vector.tensor_tensor(window[b][:].indirect(offsets[:]), shared_sb[b][:], weighted_sb[b][:], ADD)
            nc.sync.dma_start(out_blocks[b], window[b][:])
